import numpy as np
import ml_dtypes


def mxq(x, axis, fmt="e4m3"):
    dtype, down = {"e4m3": (ml_dtypes.float8_e4m3fn, 7), "e5m2": (ml_dtypes.float8_e5m2, 14)}[fmt]
    v = np.moveaxis(np.asarray(x, np.float32).astype(ml_dtypes.bfloat16).astype(np.float64), axis, -1)
    blocks = v.reshape(v.shape[:-1] + (-1, 32))
    amax = np.abs(blocks).max(-1, keepdims=True)
    byte = np.maximum(np.where(amax > 0, np.frexp(amax)[1] - 1 + 127, 0) - down, 1)
    scale = np.exp2(byte - 127.0)
    codes = (blocks / scale).astype(np.float32).astype(dtype).astype(np.float64)
    return np.moveaxis((codes * scale).reshape(v.shape), -1, axis)


WIDE = False


def mx_kscale(k):
    if not WIDE:
        return np.ones(k)
    levels = np.array([10, -10, 5, -5, 0])
    a = np.random.permutation(np.resize(levels, k // 512 * 4)).reshape(k // 512, 4)
    idx = np.arange(k)
    return np.exp2(a[idx // 512, idx % 128 // 32])


BF16 = ml_dtypes.bfloat16


def bf(x):
    return np.asarray(x, np.float32).astype(BF16)


def f64(x):
    return np.asarray(x).astype(np.float64)


B, NH, T, N = 1, 4, 1024, 512
THETA = 2.0 ** 16
STEP = 8


def rope(v, cos, sin):
    v_rot = np.stack((-v[..., 1::2], v[..., ::2]), axis=-1).reshape(v.shape)
    return v * cos + v_rot * sin


def setup_inputs():
    a, b = np.sqrt(11.0 / np.sqrt(N)), np.sqrt(1.4 / np.sqrt(N))
    q = a * np.random.standard_normal((B, NH, 1, N)) + b * np.random.standard_normal((B, NH, T, N))
    v = np.random.standard_normal((B, NH, T, N))
    omega = np.repeat(THETA ** (-np.arange(0, N, 2) / N), 2)
    phi = np.repeat(np.random.uniform(0.0, 2.0 * np.pi, N // 2), 2)
    ang = (np.arange(T)[:, None] * omega[None, :] + phi[None, :]).reshape(1, 1, T, N)
    s = mx_kscale(N)
    u = np.exp2(np.round(np.log2(s / s.max()) / 2))
    g = np.where((np.arange(T) % STEP == 0)[:, None], 1.0 / u[None, :], u[None, :]).reshape(1, 1, T, N)
    return {"Q": bf(q), "V": bf(v), "rope_cos": bf(np.cos(ang) * g), "rope_sin": bf(np.sin(ang) * g)}


def reference(Q, V, rope_cos, rope_sin):
    qr = rope(f64(Q), f64(rope_cos), f64(rope_sin))
    qrq = mxq(qr, 3, "e4m3")
    s = (qrq @ qrq.transpose(0, 1, 3, 2)) / np.sqrt(N)
    e = np.exp(s - s.max(-1, keepdims=True))
    return (mxq(e, 3, "e4m3") @ mxq(f64(V), 2, "e4m3")) / e.sum(-1, keepdims=True)

@@ -1,0 +1,207 @@
+from contextlib import ExitStack
+
+import concourse.mybir as mybir
+from concourse.masks import make_identity
+
+F32 = mybir.dt.float32
+BF16 = mybir.dt.bfloat16
+U32 = mybir.dt.uint32
+U8 = mybir.dt.uint8
+FP8X4 = mybir.dt.float8_e4m3fn_x4
+ALU = mybir.AluOpType
+ACT = mybir.ActivationFunctionType
+
+P = 128
+HEADS = 4
+T = 1024
+N = 512
+GROUPS = 4
+K_PASS = 512
+PASSES = T // K_PASS
+SCORE_SCALE = 1.0 / 512.0**0.5
+
+FLOPS = 2 * 2 * HEADS * T * T * N
+
+
+def tile_bidirectionalattentionv2_pa_t_kernel(tc, Q, V, rope_cos, rope_sin, out):
+    nc = tc.nc
+    q_rows = Q.flatten_outer_dims()
+    v_rows = V.flatten_outer_dims()
+    cos_rows = rope_cos.flatten_outer_dims()
+    sin_rows = rope_sin.flatten_outer_dims()
+    out_rows = out.flatten_outer_dims()
+
+    with ExitStack() as stack:
+        const = stack.enter_context(tc.tile_pool(name="const", bufs=1))
+        keep = stack.enter_context(tc.tile_pool(name="keep", bufs=1))
+        rope_pool = stack.enter_context(tc.tile_pool(name="rope", bufs=3))
+        grouped_pool = stack.enter_context(tc.tile_pool(name="grouped", bufs=2))
+        v_pool = stack.enter_context(tc.tile_pool(name="vgrouped", bufs=4))
+        strip_pool = stack.enter_context(tc.tile_pool(name="strip", bufs=3))
+        small = stack.enter_context(tc.tile_pool(name="small", bufs=4))
+        psum = stack.enter_context(tc.psum_pool(name="psum", bufs=2))
+
+        ident = const.tile([P, P], F32)
+        make_identity(nc, ident[:])
+
+        cos_sb = const.tile([P, GROUPS, 2, N], BF16)
+        sin_sb = const.tile([P, GROUPS, 2, N], BF16)
+        q_sb = [keep.tile([P, GROUPS, 2, N], BF16, name="q%d" % h) for h in range(HEADS)]
+        v_sb = [keep.tile([P, PASSES, 4, N], BF16, name="v%d" % h) for h in range(HEADS)]
+
+        def load_group(tile_ap, rows, first_row, b):
+            nc.sync.dma_start(
+                out=tile_ap[:, b].rearrange("p a n -> p (a n)"),
+                in_=rows[first_row + 256 * b : first_row + 256 * (b + 1), :].rearrange(
+                    "(y a) n -> y (a n)", a=2
+                ),
+            )
+
+        def load_v(h):
+            nc.sync.dma_start(
+                out=v_sb[h][:].rearrange("p g t n -> p g (t n)"),
+                in_=v_rows[h * T : (h + 1) * T, :].rearrange("(g p t) n -> p g (t n)", g=PASSES, t=4),
+            )
+
+        for b in range(GROUPS):
+            load_group(q_sb[0], q_rows, 0, b)
+            load_group(cos_sb, cos_rows, 0, b)
+            load_group(sin_sb, sin_rows, 0, b)
+        load_v(0)
+        for h in range(1, HEADS):
+            for b in range(GROUPS):
+                load_group(q_sb[h], q_rows, h * T, b)
+            load_v(h)
+
+        qr_codes = [keep.tile([P, T], U32, name="qr_codes%d" % h, align_bytes=64) for h in range(HEADS)]
+        qr_scales = [keep.tile([P, T], U8, name="qr_scales%d" % h, align_bytes=64) for h in range(HEADS)]
+        v_codes = [
+            keep.tile([P, PASSES, N], U32, name="v_codes%d" % h, align_bytes=64) for h in range(HEADS)
+        ]
+        v_scales = [
+            keep.tile([P, PASSES, N], U8, name="v_scales%d" % h, align_bytes=64) for h in range(HEADS)
+        ]
+        qr_grouped = {}
+
+        def rope_group(h, b):
+            if b == 0:
+                qr_grouped[h] = grouped_pool.tile([P, 4 * T], BF16, name="qr_grouped", align_bytes=64)
+            q_planes = q_sb[h][:, b].rearrange("p a (i e) -> p a e i", e=2)
+            cos_planes = cos_sb[:, b].rearrange("p a (i e) -> p a e i", e=2)
+            sin_planes = sin_sb[:, b].rearrange("p a (i e) -> p a e i", e=2)
+            by_cos = rope_pool.tile([P, 2, 2, N // 2], F32)
+            by_sin = rope_pool.tile([P, 2, 2, N // 2], F32)
+            qr = rope_pool.tile([P, 2, 2, N // 2], BF16)
+            cos_engine = nc.vector if h == 0 else nc.gpsimd
+            cos_engine.tensor_tensor(out=by_cos[:], in0=q_planes, in1=cos_planes, op=ALU.mult)
+            for e in range(2):
+                nc.gpsimd.tensor_tensor(
+                    out=by_sin[:, :, e, :], in0=q_planes[:, :, 1 - e, :], in1=sin_planes[:, :, e, :], op=ALU.mult
+                )
+            nc.vector.tensor_tensor(
+                out=qr[:, :, 0, :], in0=by_cos[:, :, 0, :], in1=by_sin[:, :, 0, :], op=ALU.subtract
+            )
+            nc.vector.tensor_tensor(
+                out=qr[:, :, 1, :], in0=by_cos[:, :, 1, :], in1=by_sin[:, :, 1, :], op=ALU.add
+            )
+            qr_words = qr[:].bitcast(F32)
+            qr_t = psum.tile([P, 2, 2, P], F32, tag="tr")
+            for a in range(2):
+                for e in range(2):
+                    nc.tensor.transpose(qr_t[:, a, e, :], qr_words[:, a, e, :], ident[:])
+            columns = qr_grouped[h][:].bitcast(F32).rearrange(
+                "p (g a half y e) -> p g a half y e", g=PASSES, a=2, half=2, e=2
+            )
+            nc.scalar.copy(out=columns[:, b // 2, :, b % 2], in_=qr_t[:].rearrange("p a e y -> p a y e"))
+            if b % 2 == 1:
+                g = b // 2
+                nc.vector.quantize_mx(
+                    out=qr_codes[h][:, K_PASS * g : K_PASS * (g + 1)].bitcast(FP8X4),
+                    scales=qr_scales[h][:, K_PASS * g : K_PASS * (g + 1)],
+                    in_=qr_grouped[h][:, 4 * K_PASS * g : 4 * K_PASS * (g + 1)],
+                )
+
+        def prepare_v(h, g):
+            v_grouped = v_pool.tile([P, N, 2, 2], BF16, align_bytes=64)
+            nc.scalar.copy(out=v_grouped[:], in_=v_sb[h][:, g].rearrange("p (e a) n -> p n a e", a=2))
+            nc.vector.quantize_mx(
+                out=v_codes[h][:, g, :].bitcast(FP8X4),
+                scales=v_scales[h][:, g, :],
+                in_=v_grouped[:].rearrange("p n a e -> p (n a e)"),
+            )
+
+        def attend(h, b, a, result):
+            first = K_PASS * (b // 2) + 256 * a + P * (b % 2)
+            scores = [psum.tile([P, K_PASS], F32, name="scores%d" % g) for g in range(PASSES)]
+            for g in range(PASSES):
+                nc.tensor.matmul_mx(
+                    out=scores[g][:],
+                    lhsT=qr_codes[h][:, first : first + P].bitcast(FP8X4),
+                    lhsT_scale=qr_scales[h][:, first : first + P],
+                    rhs=qr_codes[h][:, K_PASS * g : K_PASS * (g + 1)].bitcast(FP8X4),
+                    rhs_scale=qr_scales[h][:, K_PASS * g : K_PASS * (g + 1)],
+                    start=True,
+                    stop=True,
+                )
+            diff = strip_pool.tile([P, T], F32)
+            run_max = small.tile([P, PASSES], F32)
+            for g in range(PASSES):
+                nc.vector.tensor_scalar(
+                    out=diff[:, K_PASS * g : K_PASS * (g + 1)],
+                    in0=scores[g][:],
+                    scalar1=1.0,
+                    scalar2=(None if g == 0 else run_max[:, g - 1 : g]),
+                    op0=ALU.mult,
+                    op1=ALU.max,
+                    accum_out=run_max[:, g : g + 1],
+                )
+            nc.vector.tensor_scalar(
+                out=diff[:], in0=diff[:], scalar1=run_max[:, PASSES - 1 : PASSES], scalar2=None, op0=ALU.subtract
+            )
+            e_sb = strip_pool.tile([P, T], BF16)
+            row_sum = small.tile([P, 1], F32)
+            nc.scalar.activation(out=e_sb[:], in_=diff[:], func=ACT.Exp, scale=SCORE_SCALE, accum_out=row_sum[:])
+            inv_sum = small.tile([P, 1], F32)
+            nc.vector.reciprocal(out=inv_sum[:], in_=row_sum[:])
+            e_words = e_sb[:].bitcast(F32)
+            e_t = psum.tile([P, 2 * PASSES, P], F32, tag="tr")
+            for j in range(2 * PASSES):
+                nc.tensor.transpose(e_t[:, j, :], e_words[:, P * j : P * (j + 1)], ident[:])
+            e_grouped = strip_pool.tile([P, 4 * PASSES * P], BF16, align_bytes=64)
+            nc.scalar.copy(
+                out=e_grouped[:].bitcast(F32).rearrange("p (g q a) -> p g q a", g=PASSES, a=2),
+                in_=e_t[:].rearrange("p (g a) q -> p g q a", a=2),
+            )
+            e_codes = strip_pool.tile([P, PASSES * P], U32, align_bytes=64)
+            e_scales = strip_pool.tile([P, PASSES * P], U8, align_bytes=64)
+            nc.vector.quantize_mx(out=e_codes[:].bitcast(FP8X4), scales=e_scales[:], in_=e_grouped[:])
+            acc = psum.tile([P, N], F32)
+            for g in range(PASSES):
+                nc.tensor.matmul_mx(
+                    out=acc[:],
+                    lhsT=e_codes[:, P * g : P * (g + 1)].bitcast(FP8X4),
+                    lhsT_scale=e_scales[:, P * g : P * (g + 1)],
+                    rhs=v_codes[h][:, g, :].bitcast(FP8X4),
+                    rhs_scale=v_scales[h][:, g, :],
+                    start=(g == 0),
+                    stop=(g == PASSES - 1),
+                )
+            nc.scalar.activation(out=result[:, a, :], in_=acc[:], func=ACT.Copy, scale=inv_sum[:])
+
+        for b in range(GROUPS):
+            rope_group(0, b)
+        for g in range(PASSES):
+            prepare_v(0, g)
+        for h in range(HEADS):
+            for b in range(GROUPS):
+                result = strip_pool.tile([P, 2, N], F32)
+                for a in range(2):
+                    attend(h, b, a, result)
+                nc.sync.dma_start(
+                    out=out_rows[h * T + 256 * b : h * T + 256 * (b + 1), :].rearrange("(y a) n -> y (a n)", a=2),
+                    in_=result[:].rearrange("p a n -> p (a n)"),
+                )
+                if h + 1 < HEADS:
+                    rope_group(h + 1, b)
+                    if b % 2 == 1:
+                        prepare_v(h + 1, b // 2)

@@ -92,10 +92,9 @@ def tile_bidirectionalattentionv2_pa_t_kernel(tc, Q, V, rope_cos, rope_sin, out)
             by_cos = rope_pool.tile([P, 2, 2, N // 2], F32)
             by_sin = rope_pool.tile([P, 2, 2, N // 2], F32)
             qr = rope_pool.tile([P, 2, 2, N // 2], BF16)
-            cos_engine = nc.vector if h == 0 else nc.gpsimd
-            cos_engine.tensor_tensor(out=by_cos[:], in0=q_planes, in1=cos_planes, op=ALU.mult)
+            nc.vector.tensor_tensor(out=by_cos[:], in0=q_planes, in1=cos_planes, op=ALU.mult)
             for e in range(2):
-                nc.gpsimd.tensor_tensor(
+                nc.vector.tensor_tensor(
                     out=by_sin[:, :, e, :], in0=q_planes[:, :, 1 - e, :], in1=sin_planes[:, :, e, :], op=ALU.mult
                 )
             nc.vector.tensor_tensor(

@@ -40,6 +40,8 @@ def tile_bidirectionalattentionv2_pa_t_kernel(tc, Q, V, rope_cos, rope_sin, out)
         strip_pool = stack.enter_context(tc.tile_pool(name="strip", bufs=3))
         small = stack.enter_context(tc.tile_pool(name="small", bufs=4))
         psum = stack.enter_context(tc.psum_pool(name="psum", bufs=2))
+        psum_scores = stack.enter_context(tc.psum_pool(name="psum_scores", bufs=3))
+        psum_one = stack.enter_context(tc.psum_pool(name="psum_one", bufs=1))
 
         ident = const.tile([P, P], F32)
         make_identity(nc, ident[:])
@@ -68,10 +70,13 @@ def tile_bidirectionalattentionv2_pa_t_kernel(tc, Q, V, rope_cos, rope_sin, out)
             load_group(cos_sb, cos_rows, 0, b)
             load_group(sin_sb, sin_rows, 0, b)
         load_v(0)
+        for b in range(GROUPS):
+            load_group(q_sb[1], q_rows, T, b)
         for h in range(1, HEADS):
+            load_v(h)
+        for h in range(2, HEADS):
             for b in range(GROUPS):
                 load_group(q_sb[h], q_rows, h * T, b)
-            load_v(h)
 
         qr_codes = [keep.tile([P, T], U32, name="qr_codes%d" % h, align_bytes=64) for h in range(HEADS)]
         qr_scales = [keep.tile([P, T], U8, name="qr_scales%d" % h, align_bytes=64) for h in range(HEADS)]
@@ -83,35 +88,39 @@ def tile_bidirectionalattentionv2_pa_t_kernel(tc, Q, V, rope_cos, rope_sin, out)
         ]
         qr_grouped = {}
 
+        def sign_sine(b):
+            even = sin_sb[:, b].rearrange("p a (i e) -> p a e i", e=2)[:, :, 0, :]
+            nc.scalar.mul(out=even, in_=even, mul=-1.0)
+
         def rope_group(h, b):
             if b == 0:
                 qr_grouped[h] = grouped_pool.tile([P, 4 * T], BF16, name="qr_grouped", align_bytes=64)
-            q_planes = q_sb[h][:, b].rearrange("p a (i e) -> p a e i", e=2)
-            cos_planes = cos_sb[:, b].rearrange("p a (i e) -> p a e i", e=2)
-            sin_planes = sin_sb[:, b].rearrange("p a (i e) -> p a e i", e=2)
-            by_cos = rope_pool.tile([P, 2, 2, N // 2], F32)
-            by_sin = rope_pool.tile([P, 2, 2, N // 2], F32)
-            qr = rope_pool.tile([P, 2, 2, N // 2], BF16)
+            q_planes = q_sb[h][:, b].rearrange("p a (w t) -> p a t w", t=4)
+            cos_planes = cos_sb[:, b].rearrange("p a (w t) -> p a t w", t=4)
+            sin_planes = sin_sb[:, b].rearrange("p a (w t) -> p a t w", t=4)
+            by_cos = rope_pool.tile([P, 2, 4, P], F32)
+            by_sin = rope_pool.tile([P, 2, 4, P], F32)
             nc.vector.tensor_tensor(out=by_cos[:], in0=q_planes, in1=cos_planes, op=ALU.mult)
             for e in range(2):
                 nc.vector.tensor_tensor(
-                    out=by_sin[:, :, e, :], in0=q_planes[:, :, 1 - e, :], in1=sin_planes[:, :, e, :], op=ALU.mult
+                    out=by_sin[:, :, e::2, :],
+                    in0=q_planes[:, :, 1 - e :: 2, :],
+                    in1=sin_planes[:, :, e::2, :],
+                    op=ALU.mult,
                 )
-            nc.vector.tensor_tensor(
-                out=qr[:, :, 0, :], in0=by_cos[:, :, 0, :], in1=by_sin[:, :, 0, :], op=ALU.subtract
+            columns = qr_grouped[h][:].rearrange(
+                "p (g a half y t) -> p g a half y t", g=PASSES, a=2, half=2, t=4
             )
-            nc.vector.tensor_tensor(
-                out=qr[:, :, 1, :], in0=by_cos[:, :, 1, :], in1=by_sin[:, :, 1, :], op=ALU.add
-            )
-            qr_words = qr[:].bitcast(F32)
-            qr_t = psum.tile([P, 2, 2, P], F32, tag="tr")
             for a in range(2):
-                for e in range(2):
-                    nc.tensor.transpose(qr_t[:, a, e, :], qr_words[:, a, e, :], ident[:])
-            columns = qr_grouped[h][:].bitcast(F32).rearrange(
-                "p (g a half y e) -> p g a half y e", g=PASSES, a=2, half=2, e=2
-            )
-            nc.scalar.copy(out=columns[:, b // 2, :, b % 2], in_=qr_t[:].rearrange("p a e y -> p a y e"))
+                qr_t = psum_one.tile([P, 4, P], F32)
+                for t in range(4):
+                    nc.tensor.matmul(
+                        out=qr_t[:, t, :], lhsT=by_cos[:, a, t, :], rhs=ident[:], start=True, stop=False, is_transpose=True
+                    )
+                    nc.tensor.matmul(
+                        out=qr_t[:, t, :], lhsT=by_sin[:, a, t, :], rhs=ident[:], start=False, stop=True, is_transpose=True
+                    )
+                nc.scalar.copy(out=columns[:, b // 2, a, b % 2], in_=qr_t[:].rearrange("p t y -> p y t"))
             if b % 2 == 1:
                 g = b // 2
                 nc.vector.quantize_mx(
@@ -131,7 +140,7 @@ def tile_bidirectionalattentionv2_pa_t_kernel(tc, Q, V, rope_cos, rope_sin, out)
 
         def attend(h, b, a, result):
             first = K_PASS * (b // 2) + 256 * a + P * (b % 2)
-            scores = [psum.tile([P, K_PASS], F32, name="scores%d" % g) for g in range(PASSES)]
+            scores = [psum_scores.tile([P, K_PASS], F32, name="scores") for g in range(PASSES)]
             for g in range(PASSES):
                 nc.tensor.matmul_mx(
                     out=scores[g][:],
@@ -142,28 +151,32 @@ def tile_bidirectionalattentionv2_pa_t_kernel(tc, Q, V, rope_cos, rope_sin, out)
                     start=True,
                     stop=True,
                 )
-            diff = strip_pool.tile([P, T], F32)
-            run_max = small.tile([P, PASSES], F32)
+            neg_s = strip_pool.tile([P, T], F32)
+            run_min = small.tile([P, PASSES], F32)
             for g in range(PASSES):
                 nc.vector.tensor_scalar(
-                    out=diff[:, K_PASS * g : K_PASS * (g + 1)],
+                    out=neg_s[:, K_PASS * g : K_PASS * (g + 1)],
                     in0=scores[g][:],
-                    scalar1=1.0,
-                    scalar2=(None if g == 0 else run_max[:, g - 1 : g]),
+                    scalar1=-SCORE_SCALE,
+                    scalar2=(None if g == 0 else run_min[:, g - 1 : g]),
                     op0=ALU.mult,
-                    op1=ALU.max,
-                    accum_out=run_max[:, g : g + 1],
+                    op1=ALU.min,
+                    accum_out=run_min[:, g : g + 1],
                 )
-            nc.vector.tensor_scalar(
-                out=diff[:], in0=diff[:], scalar1=run_max[:, PASSES - 1 : PASSES], scalar2=None, op0=ALU.subtract
-            )
             e_sb = strip_pool.tile([P, T], BF16)
             row_sum = small.tile([P, 1], F32)
-            nc.scalar.activation(out=e_sb[:], in_=diff[:], func=ACT.Exp, scale=SCORE_SCALE, accum_out=row_sum[:])
+            nc.scalar.activation(
+                out=e_sb[:],
+                in_=neg_s[:],
+                func=ACT.Exp,
+                bias=run_min[:, PASSES - 1 : PASSES],
+                scale=-1.0,
+                accum_out=row_sum[:],
+            )
             inv_sum = small.tile([P, 1], F32)
             nc.vector.reciprocal(out=inv_sum[:], in_=row_sum[:])
             e_words = e_sb[:].bitcast(F32)
-            e_t = psum.tile([P, 2 * PASSES, P], F32, tag="tr")
+            e_t = psum.tile([P, 2 * PASSES, P], F32)
             for j in range(2 * PASSES):
                 nc.tensor.transpose(e_t[:, j, :], e_words[:, P * j : P * (j + 1)], ident[:])
             e_grouped = strip_pool.tile([P, 4 * PASSES * P], BF16, align_bytes=64)
@@ -185,12 +198,19 @@ def tile_bidirectionalattentionv2_pa_t_kernel(tc, Q, V, rope_cos, rope_sin, out)
                     start=(g == 0),
                     stop=(g == PASSES - 1),
                 )
-            nc.scalar.activation(out=result[:, a, :], in_=acc[:], func=ACT.Copy, scale=inv_sum[:])
+            if a == 0:
+                nc.scalar.activation(out=result[:, a, :], in_=acc[:], func=ACT.Copy, scale=inv_sum[:])
+            else:
+                nc.vector.tensor_scalar(
+                    out=result[:, a, :], in0=acc[:], scalar1=inv_sum[:], scalar2=None, op0=ALU.mult
+                )
 
         for b in range(GROUPS):
+            sign_sine(b)
             rope_group(0, b)
-        for g in range(PASSES):
-            prepare_v(0, g)
+        for h in range(HEADS):
+            for g in range(PASSES):
+                prepare_v(h, g)
         for h in range(HEADS):
             for b in range(GROUPS):
                 result = strip_pool.tile([P, 2, N], F32)
@@ -202,5 +222,3 @@ def tile_bidirectionalattentionv2_pa_t_kernel(tc, Q, V, rope_cos, rope_sin, out)
                 )
                 if h + 1 < HEADS:
                     rope_group(h + 1, b)
-                    if b % 2 == 1:
-                        prepare_v(h + 1, b // 2)

@@ -19,6 +19,12 @@ GROUPS = 4
 K_PASS = 512
 PASSES = T // K_PASS
 SCORE_SCALE = 1.0 / 512.0**0.5
+TILES = T // P
+STRIPS = HEADS * TILES
+
+ROPE_STAGES = 4
+ROPE_LEAD = TILES - 1 + ROPE_STAGES
+STRIP_STAGES = 8
 
 FLOPS = 2 * 2 * HEADS * T * T * N
 
@@ -36,12 +42,12 @@ def tile_bidirectionalattentionv2_pa_t_kernel(tc, Q, V, rope_cos, rope_sin, out)
         keep = stack.enter_context(tc.tile_pool(name="keep", bufs=1))
         rope_pool = stack.enter_context(tc.tile_pool(name="rope", bufs=3))
         grouped_pool = stack.enter_context(tc.tile_pool(name="grouped", bufs=2))
-        v_pool = stack.enter_context(tc.tile_pool(name="vgrouped", bufs=4))
         strip_pool = stack.enter_context(tc.tile_pool(name="strip", bufs=3))
-        small = stack.enter_context(tc.tile_pool(name="small", bufs=4))
-        psum = stack.enter_context(tc.psum_pool(name="psum", bufs=2))
-        psum_scores = stack.enter_context(tc.psum_pool(name="psum_scores", bufs=3))
-        psum_one = stack.enter_context(tc.psum_pool(name="psum_one", bufs=1))
+        small = stack.enter_context(tc.tile_pool(name="small", bufs=8))
+        psum_scores = stack.enter_context(tc.psum_pool(name="psum_scores", bufs=4))
+        psum_turned = stack.enter_context(tc.psum_pool(name="psum_turned", bufs=3))
+        psum_acc = stack.enter_context(tc.psum_pool(name="psum_acc", bufs=1))
+        stack.enter_context(tc.manual_schedule())
 
         ident = const.tile([P, P], F32)
         make_identity(nc, ident[:])
@@ -69,14 +75,11 @@ def tile_bidirectionalattentionv2_pa_t_kernel(tc, Q, V, rope_cos, rope_sin, out)
             load_group(q_sb[0], q_rows, 0, b)
             load_group(cos_sb, cos_rows, 0, b)
             load_group(sin_sb, sin_rows, 0, b)
-        load_v(0)
-        for b in range(GROUPS):
-            load_group(q_sb[1], q_rows, T, b)
-        for h in range(1, HEADS):
+        for h in range(HEADS):
+            if h + 1 < HEADS:
+                for b in range(GROUPS):
+                    load_group(q_sb[h + 1], q_rows, (h + 1) * T, b)
             load_v(h)
-        for h in range(2, HEADS):
-            for b in range(GROUPS):
-                load_group(q_sb[h], q_rows, h * T, b)
 
         qr_codes = [keep.tile([P, T], U32, name="qr_codes%d" % h, align_bytes=64) for h in range(HEADS)]
         qr_scales = [keep.tile([P, T], U8, name="qr_scales%d" % h, align_bytes=64) for h in range(HEADS)]
@@ -86,42 +89,56 @@ def tile_bidirectionalattentionv2_pa_t_kernel(tc, Q, V, rope_cos, rope_sin, out)
         v_scales = [
             keep.tile([P, PASSES, N], U8, name="v_scales%d" % h, align_bytes=64) for h in range(HEADS)
         ]
+
+        def place(i):
+            return i // TILES, (i % TILES) // 2, i % 2
+
+        products = {}
+        qr_turned = {}
         qr_grouped = {}
 
         def sign_sine(b):
             even = sin_sb[:, b].rearrange("p a (i e) -> p a e i", e=2)[:, :, 0, :]
             nc.scalar.mul(out=even, in_=even, mul=-1.0)
 
-        def rope_group(h, b):
-            if b == 0:
-                qr_grouped[h] = grouped_pool.tile([P, 4 * T], BF16, name="qr_grouped", align_bytes=64)
-            q_planes = q_sb[h][:, b].rearrange("p a (w t) -> p a t w", t=4)
-            cos_planes = cos_sb[:, b].rearrange("p a (w t) -> p a t w", t=4)
-            sin_planes = sin_sb[:, b].rearrange("p a (w t) -> p a t w", t=4)
-            by_cos = rope_pool.tile([P, 2, 4, P], F32)
-            by_sin = rope_pool.tile([P, 2, 4, P], F32)
+        def rope_products(i):
+            h, b, a = place(i)
+            q_planes = q_sb[h][:, b, a].rearrange("p (w t) -> p t w", t=4)
+            cos_planes = cos_sb[:, b, a].rearrange("p (w t) -> p t w", t=4)
+            sin_planes = sin_sb[:, b, a].rearrange("p (w t) -> p t w", t=4)
+            by_cos = rope_pool.tile([P, 4, P], F32)
+            by_sin = rope_pool.tile([P, 4, P], F32)
             nc.vector.tensor_tensor(out=by_cos[:], in0=q_planes, in1=cos_planes, op=ALU.mult)
             for e in range(2):
                 nc.vector.tensor_tensor(
-                    out=by_sin[:, :, e::2, :],
-                    in0=q_planes[:, :, 1 - e :: 2, :],
-                    in1=sin_planes[:, :, e::2, :],
-                    op=ALU.mult,
+                    out=by_sin[:, e::2, :], in0=q_planes[:, 1 - e :: 2, :], in1=sin_planes[:, e::2, :], op=ALU.mult
                 )
+            products[i] = (by_cos, by_sin)
+
+        def rope_transpose(i):
+            by_cos, by_sin = products[i]
+            turned = psum_turned.tile([P, 4, P], F32, name="turned")
+            for t in range(4):
+                nc.tensor.matmul(
+                    out=turned[:, t, :], lhsT=by_cos[:, t, :], rhs=ident[:], start=True, stop=False, is_transpose=True
+                )
+                nc.tensor.matmul(
+                    out=turned[:, t, :], lhsT=by_sin[:, t, :], rhs=ident[:], start=False, stop=True, is_transpose=True
+                )
+            qr_turned[i] = turned
+
+        def rope_group(i):
+            h, b, a = place(i)
+            if i % TILES == 0:
+                qr_grouped[h] = grouped_pool.tile([P, 4 * T], BF16, name="qr_grouped", align_bytes=64)
             columns = qr_grouped[h][:].rearrange(
                 "p (g a half y t) -> p g a half y t", g=PASSES, a=2, half=2, t=4
             )
-            for a in range(2):
-                qr_t = psum_one.tile([P, 4, P], F32)
-                for t in range(4):
-                    nc.tensor.matmul(
-                        out=qr_t[:, t, :], lhsT=by_cos[:, a, t, :], rhs=ident[:], start=True, stop=False, is_transpose=True
-                    )
-                    nc.tensor.matmul(
-                        out=qr_t[:, t, :], lhsT=by_sin[:, a, t, :], rhs=ident[:], start=False, stop=True, is_transpose=True
-                    )
-                nc.scalar.copy(out=columns[:, b // 2, a, b % 2], in_=qr_t[:].rearrange("p t y -> p y t"))
-            if b % 2 == 1:
+            nc.scalar.copy(out=columns[:, b // 2, a, b % 2], in_=qr_turned[i][:].rearrange("p t y -> p y t"))
+
+        def rope_quantise(i):
+            h, b, a = place(i)
+            if (b % 2, a) == (1, 1):
                 g = b // 2
                 nc.vector.quantize_mx(
                     out=qr_codes[h][:, K_PASS * g : K_PASS * (g + 1)].bitcast(FP8X4),
@@ -129,21 +146,38 @@ def tile_bidirectionalattentionv2_pa_t_kernel(tc, Q, V, rope_cos, rope_sin, out)
                     in_=qr_grouped[h][:, 4 * K_PASS * g : 4 * K_PASS * (g + 1)],
                 )
 
-        def prepare_v(h, g):
-            v_grouped = v_pool.tile([P, N, 2, 2], BF16, align_bytes=64)
-            nc.scalar.copy(out=v_grouped[:], in_=v_sb[h][:, g].rearrange("p (e a) n -> p n a e", a=2))
+        v_grouped = {}
+
+        def v_group(h, g):
+            v_grouped[h, g] = grouped_pool.tile([P, N, 2, 2], BF16, name="v_grouped", align_bytes=64)
+            nc.vector.tensor_copy(out=v_grouped[h, g][:], in_=v_sb[h][:, g].rearrange("p (e a) n -> p n a e", a=2))
+
+        def v_quantise(h, g):
             nc.vector.quantize_mx(
                 out=v_codes[h][:, g, :].bitcast(FP8X4),
                 scales=v_scales[h][:, g, :],
-                in_=v_grouped[:].rearrange("p n a e -> p (n a e)"),
+                in_=v_grouped[h, g][:].rearrange("p n a e -> p (n a e)"),
             )
 
-        def attend(h, b, a, result):
+        scores = {}
+        neg_s = {}
+        run_min = {}
+        e_sb = {}
+        row_sum = {}
+        e_turned = {}
+        e_grouped = {}
+        e_operand = {}
+        inv_sum = {}
+        acc = {}
+        result = {}
+
+        def strip_scores(i):
+            h, b, a = place(i)
             first = K_PASS * (b // 2) + 256 * a + P * (b % 2)
-            scores = [psum_scores.tile([P, K_PASS], F32, name="scores") for g in range(PASSES)]
+            scores[i] = [psum_scores.tile([P, K_PASS], F32, name="scores") for g in range(PASSES)]
             for g in range(PASSES):
                 nc.tensor.matmul_mx(
-                    out=scores[g][:],
+                    out=scores[i][g][:],
                     lhsT=qr_codes[h][:, first : first + P].bitcast(FP8X4),
                     lhsT_scale=qr_scales[h][:, first : first + P],
                     rhs=qr_codes[h][:, K_PASS * g : K_PASS * (g + 1)].bitcast(FP8X4),
@@ -151,46 +185,61 @@ def tile_bidirectionalattentionv2_pa_t_kernel(tc, Q, V, rope_cos, rope_sin, out)
                     start=True,
                     stop=True,
                 )
-            neg_s = strip_pool.tile([P, T], F32)
-            run_min = small.tile([P, PASSES], F32)
-            for g in range(PASSES):
-                nc.vector.tensor_scalar(
-                    out=neg_s[:, K_PASS * g : K_PASS * (g + 1)],
-                    in0=scores[g][:],
-                    scalar1=-SCORE_SCALE,
-                    scalar2=(None if g == 0 else run_min[:, g - 1 : g]),
-                    op0=ALU.mult,
-                    op1=ALU.min,
-                    accum_out=run_min[:, g : g + 1],
-                )
-            e_sb = strip_pool.tile([P, T], BF16)
-            row_sum = small.tile([P, 1], F32)
+
+        def strip_max(i, g):
+            if g == 0:
+                neg_s[i] = strip_pool.tile([P, T], F32, name="neg_s")
+                run_min[i] = small.tile([P, PASSES], F32, name="run_min")
+            nc.vector.tensor_scalar(
+                out=neg_s[i][:, K_PASS * g : K_PASS * (g + 1)],
+                in0=scores[i][g][:],
+                scalar1=-SCORE_SCALE,
+                scalar2=(None if g == 0 else run_min[i][:, g - 1 : g]),
+                op0=ALU.mult,
+                op1=ALU.min,
+                accum_out=run_min[i][:, g : g + 1],
+            )
+
+        def strip_exp(i):
+            e_sb[i] = strip_pool.tile([P, T], BF16, name="e_sb")
+            row_sum[i] = small.tile([P, 1], F32, name="row_sum")
             nc.scalar.activation(
-                out=e_sb[:],
-                in_=neg_s[:],
+                out=e_sb[i][:],
+                in_=neg_s[i][:],
                 func=ACT.Exp,
-                bias=run_min[:, PASSES - 1 : PASSES],
+                bias=run_min[i][:, PASSES - 1 : PASSES],
                 scale=-1.0,
-                accum_out=row_sum[:],
+                accum_out=row_sum[i][:],
             )
-            inv_sum = small.tile([P, 1], F32)
-            nc.vector.reciprocal(out=inv_sum[:], in_=row_sum[:])
-            e_words = e_sb[:].bitcast(F32)
-            e_t = psum.tile([P, 2 * PASSES, P], F32)
+
+        def strip_transpose(i):
+            e_words = e_sb[i][:].bitcast(F32)
+            e_turned[i] = psum_turned.tile([P, 2 * PASSES, P], F32, name="turned")
             for j in range(2 * PASSES):
-                nc.tensor.transpose(e_t[:, j, :], e_words[:, P * j : P * (j + 1)], ident[:])
-            e_grouped = strip_pool.tile([P, 4 * PASSES * P], BF16, align_bytes=64)
+                nc.tensor.transpose(e_turned[i][:, j, :], e_words[:, P * j : P * (j + 1)], ident[:])
+
+        def strip_group(i):
+            e_grouped[i] = strip_pool.tile([P, 4 * PASSES * P], BF16, name="e_grouped", align_bytes=64)
             nc.scalar.copy(
-                out=e_grouped[:].bitcast(F32).rearrange("p (g q a) -> p g q a", g=PASSES, a=2),
-                in_=e_t[:].rearrange("p (g a) q -> p g q a", a=2),
+                out=e_grouped[i][:].bitcast(F32).rearrange("p (g q a) -> p g q a", g=PASSES, a=2),
+                in_=e_turned[i][:].rearrange("p (g a) q -> p g q a", a=2),
             )
+
+        def strip_quantise(i):
             e_codes = strip_pool.tile([P, PASSES * P], U32, align_bytes=64)
             e_scales = strip_pool.tile([P, PASSES * P], U8, align_bytes=64)
-            nc.vector.quantize_mx(out=e_codes[:].bitcast(FP8X4), scales=e_scales[:], in_=e_grouped[:])
-            acc = psum.tile([P, N], F32)
+            nc.vector.quantize_mx(out=e_codes[:].bitcast(FP8X4), scales=e_scales[:], in_=e_grouped[i][:])
+            e_operand[i] = (e_codes, e_scales)
+            inv_sum[i] = small.tile([P, 1], F32, name="inv_sum")
+            nc.vector.reciprocal(out=inv_sum[i][:], in_=row_sum[i][:])
+
+        def strip_values(i):
+            h, b, a = place(i)
+            e_codes, e_scales = e_operand[i]
+            acc[i] = psum_acc.tile([P, N], F32, name="acc")
             for g in range(PASSES):
                 nc.tensor.matmul_mx(
-                    out=acc[:],
+                    out=acc[i][:],
                     lhsT=e_codes[:, P * g : P * (g + 1)].bitcast(FP8X4),
                     lhsT_scale=e_scales[:, P * g : P * (g + 1)],
                     rhs=v_codes[h][:, g, :].bitcast(FP8X4),
@@ -198,27 +247,53 @@ def tile_bidirectionalattentionv2_pa_t_kernel(tc, Q, V, rope_cos, rope_sin, out)
                     start=(g == 0),
                     stop=(g == PASSES - 1),
                 )
-            if a == 0:
-                nc.scalar.activation(out=result[:, a, :], in_=acc[:], func=ACT.Copy, scale=inv_sum[:])
-            else:
-                nc.vector.tensor_scalar(
-                    out=result[:, a, :], in0=acc[:], scalar1=inv_sum[:], scalar2=None, op0=ALU.mult
-                )
 
-        for b in range(GROUPS):
-            sign_sine(b)
-            rope_group(0, b)
-        for h in range(HEADS):
-            for g in range(PASSES):
-                prepare_v(h, g)
-        for h in range(HEADS):
-            for b in range(GROUPS):
-                result = strip_pool.tile([P, 2, N], F32)
-                for a in range(2):
-                    attend(h, b, a, result)
+        def strip_out(i):
+            h, b, a = place(i)
+            if a == 0:
+                result[h, b] = strip_pool.tile([P, 2, N], F32, name="result")
+            nc.scalar.activation(out=result[h, b][:, a, :], in_=acc[i][:], func=ACT.Copy, scale=inv_sum[i][:])
+            if a == 1:
                 nc.sync.dma_start(
                     out=out_rows[h * T + 256 * b : h * T + 256 * (b + 1), :].rearrange("(y a) n -> y (a n)", a=2),
-                    in_=result[:].rearrange("p a n -> p (a n)"),
+                    in_=result[h, b][:].rearrange("p a n -> p (a n)"),
                 )
-                if h + 1 < HEADS:
-                    rope_group(h + 1, b)
+
+        def is_strip(i):
+            return 0 <= i < STRIPS
+
+        for r in range(-ROPE_LEAD, STRIPS + STRIP_STAGES - 1):
+            tile_i = r + ROPE_LEAD
+            if tile_i < TILES and tile_i % 2 == 0:
+                sign_sine(tile_i // 2)
+            if is_strip(r - 7):
+                strip_out(r - 7)
+            if is_strip(r - 4):
+                strip_group(r - 4)
+            if is_strip(tile_i - 2):
+                rope_group(tile_i - 2)
+            if is_strip(r - 1):
+                strip_max(r - 1, 0)
+            if is_strip(r - 5):
+                strip_quantise(r - 5)
+            if is_strip(r - 1):
+                strip_max(r - 1, 1)
+            if is_strip(r - 2):
+                strip_exp(r - 2)
+            if is_strip(tile_i - 3):
+                rope_quantise(tile_i - 3)
+            if is_strip(tile_i):
+                rope_products(tile_i)
+            for g in range(PASSES):
+                if is_strip(r) and r % TILES == 2 * g:
+                    v_group(r // TILES, g)
+                if is_strip(r) and r % TILES == 2 * g + 1:
+                    v_quantise(r // TILES, g)
+            if is_strip(r):
+                strip_scores(r)
+            if is_strip(r - 6):
+                strip_values(r - 6)
+            if is_strip(r - 3):
+                strip_transpose(r - 3)
+            if is_strip(tile_i - 1):
+                rope_transpose(tile_i - 1)

@@ -103,15 +103,20 @@ def tile_bidirectionalattentionv2_pa_t_kernel(tc, Q, V, rope_cos, rope_sin, out)
 
         def rope_products(i):
             h, b, a = place(i)
-            q_planes = q_sb[h][:, b, a].rearrange("p (w t) -> p t w", t=4)
-            cos_planes = cos_sb[:, b, a].rearrange("p (w t) -> p t w", t=4)
-            sin_planes = sin_sb[:, b, a].rearrange("p (w t) -> p t w", t=4)
+            q_blocks = q_sb[h][:, b, a].rearrange("p (k i t) -> p k t i", i=4, t=4)
+            cos_blocks = cos_sb[:, b, a].rearrange("p (k i t) -> p k t i", i=4, t=4)
+            sin_blocks = sin_sb[:, b, a].rearrange("p (k i t) -> p k t i", i=4, t=4)
             by_cos = rope_pool.tile([P, 4, P], F32)
             by_sin = rope_pool.tile([P, 4, P], F32)
-            nc.vector.tensor_tensor(out=by_cos[:], in0=q_planes, in1=cos_planes, op=ALU.mult)
+            by_cos_blocks = by_cos[:].rearrange("p t (k i) -> p k t i", i=4)
+            by_sin_blocks = by_sin[:].rearrange("p t (k i) -> p k t i", i=4)
+            nc.vector.tensor_tensor(out=by_cos_blocks, in0=q_blocks, in1=cos_blocks, op=ALU.mult)
             for e in range(2):
                 nc.vector.tensor_tensor(
-                    out=by_sin[:, e::2, :], in0=q_planes[:, 1 - e :: 2, :], in1=sin_planes[:, e::2, :], op=ALU.mult
+                    out=by_sin_blocks[:, :, e::2, :],
+                    in0=q_blocks[:, :, 1 - e :: 2, :],
+                    in1=sin_blocks[:, :, e::2, :],
+                    op=ALU.mult,
                 )
             products[i] = (by_cos, by_sin)
 

@@ -26,6 +26,8 @@ ROPE_STAGES = 4
 ROPE_LEAD = TILES - 1 + ROPE_STAGES
 STRIP_STAGES = 8
 
+GPSIMD_FROM = ROPE_LEAD + 5
+
 FLOPS = 2 * 2 * HEADS * T * T * N
 
 
@@ -106,11 +108,16 @@ def tile_bidirectionalattentionv2_pa_t_kernel(tc, Q, V, rope_cos, rope_sin, out)
             q_blocks = q_sb[h][:, b, a].rearrange("p (k i t) -> p k t i", i=4, t=4)
             cos_blocks = cos_sb[:, b, a].rearrange("p (k i t) -> p k t i", i=4, t=4)
             sin_blocks = sin_sb[:, b, a].rearrange("p (k i t) -> p k t i", i=4, t=4)
-            by_cos = rope_pool.tile([P, 4, P], F32)
+            if i < GPSIMD_FROM:
+                cos_engine = nc.vector
+                by_cos = rope_pool.tile([P, 4, P], F32, name="by_cos")
+            else:
+                cos_engine = nc.gpsimd
+                by_cos = strip_pool.tile([P, 4, P], F32, name="by_cos_shared", tag="shared", align_bytes=64)
             by_sin = rope_pool.tile([P, 4, P], F32)
             by_cos_blocks = by_cos[:].rearrange("p t (k i) -> p k t i", i=4)
             by_sin_blocks = by_sin[:].rearrange("p t (k i) -> p k t i", i=4)
-            nc.vector.tensor_tensor(out=by_cos_blocks, in0=q_blocks, in1=cos_blocks, op=ALU.mult)
+            cos_engine.tensor_tensor(out=by_cos_blocks, in0=q_blocks, in1=cos_blocks, op=ALU.mult)
             for e in range(2):
                 nc.vector.tensor_tensor(
                     out=by_sin_blocks[:, :, e::2, :],
@@ -224,7 +231,7 @@ def tile_bidirectionalattentionv2_pa_t_kernel(tc, Q, V, rope_cos, rope_sin, out)
                 nc.tensor.transpose(e_turned[i][:, j, :], e_words[:, P * j : P * (j + 1)], ident[:])
 
         def strip_group(i):
-            e_grouped[i] = strip_pool.tile([P, 4 * PASSES * P], BF16, name="e_grouped", align_bytes=64)
+            e_grouped[i] = strip_pool.tile([P, 4 * PASSES * P], BF16, name="e_grouped", tag="shared", align_bytes=64)
             nc.scalar.copy(
                 out=e_grouped[i][:].bitcast(F32).rearrange("p (g q a) -> p g q a", g=PASSES, a=2),
                 in_=e_turned[i][:].rearrange("p (g a) q -> p g q a", a=2),
@@ -235,6 +242,8 @@ def tile_bidirectionalattentionv2_pa_t_kernel(tc, Q, V, rope_cos, rope_sin, out)
             e_scales = strip_pool.tile([P, PASSES * P], U8, align_bytes=64)
             nc.vector.quantize_mx(out=e_codes[:].bitcast(FP8X4), scales=e_scales[:], in_=e_grouped[i][:])
             e_operand[i] = (e_codes, e_scales)
+
+        def strip_inverse(i):
             inv_sum[i] = small.tile([P, 1], F32, name="inv_sum")
             nc.vector.reciprocal(out=inv_sum[i][:], in_=row_sum[i][:])
 
@@ -277,12 +286,14 @@ def tile_bidirectionalattentionv2_pa_t_kernel(tc, Q, V, rope_cos, rope_sin, out)
                 strip_group(r - 4)
             if is_strip(tile_i - 2):
                 rope_group(tile_i - 2)
+            if is_strip(r - 5):
+                strip_quantise(r - 5)
+            if is_strip(r - 2):
+                strip_max(r - 2, 1)
             if is_strip(r - 1):
                 strip_max(r - 1, 0)
             if is_strip(r - 5):
-                strip_quantise(r - 5)
-            if is_strip(r - 1):
-                strip_max(r - 1, 1)
+                strip_inverse(r - 5)
             if is_strip(r - 2):
                 strip_exp(r - 2)
             if is_strip(tile_i - 3):

@@ -26,7 +26,13 @@ ROPE_STAGES = 4
 ROPE_LEAD = TILES - 1 + ROPE_STAGES
 STRIP_STAGES = 8
 
-GPSIMD_FROM = ROPE_LEAD + 5
+EARLY_V = 2
+V_ROUND = -7
+
+GPSIMD_FROM = ROPE_LEAD + 1
+E_SHARED_FROM = ROPE_LEAD + 5
+V_PIECE_ROUND = STRIPS - ROPE_LEAD
+V_PIECES = 4
 
 FLOPS = 2 * 2 * HEADS * T * T * N
 
@@ -44,11 +50,12 @@ def tile_bidirectionalattentionv2_pa_t_kernel(tc, Q, V, rope_cos, rope_sin, out)
         keep = stack.enter_context(tc.tile_pool(name="keep", bufs=1))
         rope_pool = stack.enter_context(tc.tile_pool(name="rope", bufs=3))
         grouped_pool = stack.enter_context(tc.tile_pool(name="grouped", bufs=2))
+        v_pool = stack.enter_context(tc.tile_pool(name="v_grouped", bufs=4))
         strip_pool = stack.enter_context(tc.tile_pool(name="strip", bufs=3))
         small = stack.enter_context(tc.tile_pool(name="small", bufs=8))
         psum_scores = stack.enter_context(tc.psum_pool(name="psum_scores", bufs=4))
-        psum_turned = stack.enter_context(tc.psum_pool(name="psum_turned", bufs=3))
-        psum_acc = stack.enter_context(tc.psum_pool(name="psum_acc", bufs=1))
+        psum_turned = stack.enter_context(tc.psum_pool(name="psum_turned", bufs=2))
+        psum_acc = stack.enter_context(tc.psum_pool(name="psum_acc", bufs=2))
         stack.enter_context(tc.manual_schedule())
 
         ident = const.tile([P, P], F32)
@@ -67,21 +74,23 @@ def tile_bidirectionalattentionv2_pa_t_kernel(tc, Q, V, rope_cos, rope_sin, out)
                 ),
             )
 
-        def load_v(h):
+        def load_v(h, g):
             nc.sync.dma_start(
-                out=v_sb[h][:].rearrange("p g t n -> p g (t n)"),
-                in_=v_rows[h * T : (h + 1) * T, :].rearrange("(g p t) n -> p g (t n)", g=PASSES, t=4),
+                out=v_sb[h][:, g].rearrange("p t n -> p (t n)"),
+                in_=v_rows[h * T + K_PASS * g : h * T + K_PASS * (g + 1), :].rearrange("(p t) n -> p (t n)", t=4),
             )
 
         for b in range(GROUPS):
             load_group(q_sb[0], q_rows, 0, b)
             load_group(cos_sb, cos_rows, 0, b)
             load_group(sin_sb, sin_rows, 0, b)
-        for h in range(HEADS):
-            if h + 1 < HEADS:
-                for b in range(GROUPS):
-                    load_group(q_sb[h + 1], q_rows, (h + 1) * T, b)
-            load_v(h)
+            if 1 <= b <= PASSES:
+                load_v(0, b - 1)
+        for h in range(1, HEADS):
+            for b in range(GROUPS):
+                load_group(q_sb[h], q_rows, h * T, b)
+                if b < PASSES:
+                    load_v(h, b)
 
         qr_codes = [keep.tile([P, T], U32, name="qr_codes%d" % h, align_bytes=64) for h in range(HEADS)]
         qr_scales = [keep.tile([P, T], U8, name="qr_scales%d" % h, align_bytes=64) for h in range(HEADS)]
@@ -99,10 +108,6 @@ def tile_bidirectionalattentionv2_pa_t_kernel(tc, Q, V, rope_cos, rope_sin, out)
         qr_turned = {}
         qr_grouped = {}
 
-        def sign_sine(b):
-            even = sin_sb[:, b].rearrange("p a (i e) -> p a e i", e=2)[:, :, 0, :]
-            nc.scalar.mul(out=even, in_=even, mul=-1.0)
-
         def rope_products(i):
             h, b, a = place(i)
             q_blocks = q_sb[h][:, b, a].rearrange("p (k i t) -> p k t i", i=4, t=4)
@@ -113,18 +118,28 @@ def tile_bidirectionalattentionv2_pa_t_kernel(tc, Q, V, rope_cos, rope_sin, out)
                 by_cos = rope_pool.tile([P, 4, P], F32, name="by_cos")
             else:
                 cos_engine = nc.gpsimd
-                by_cos = strip_pool.tile([P, 4, P], F32, name="by_cos_shared", tag="shared", align_bytes=64)
+                pool, tag = (v_pool, "v_grouped") if i < E_SHARED_FROM else (strip_pool, "shared")
+                by_cos = pool.tile([P, 4, P], F32, name="by_cos_" + tag, tag=tag, align_bytes=64)
             by_sin = rope_pool.tile([P, 4, P], F32)
             by_cos_blocks = by_cos[:].rearrange("p t (k i) -> p k t i", i=4)
             by_sin_blocks = by_sin[:].rearrange("p t (k i) -> p k t i", i=4)
             cos_engine.tensor_tensor(out=by_cos_blocks, in0=q_blocks, in1=cos_blocks, op=ALU.mult)
-            for e in range(2):
-                nc.vector.tensor_tensor(
-                    out=by_sin_blocks[:, :, e::2, :],
-                    in0=q_blocks[:, :, 1 - e :: 2, :],
-                    in1=sin_blocks[:, :, e::2, :],
-                    op=ALU.mult,
-                )
+            nc.vector.tensor_tensor(
+                out=by_sin_blocks[:, :, 1::2, :],
+                in0=q_blocks[:, :, 0::2, :],
+                in1=sin_blocks[:, :, 1::2, :],
+                op=ALU.mult,
+            )
+            q_planes = q_sb[h][:, b, a].rearrange("p (w t) -> p t w", t=4)
+            sin_planes = sin_sb[:, b, a].rearrange("p (w t) -> p t w", t=4)
+            nc.vector.scalar_tensor_tensor(
+                out=by_sin[:, 0::2, :],
+                in0=q_planes[:, 1::2, :],
+                scalar=-1.0,
+                in1=sin_planes[:, 0::2, :],
+                op0=ALU.mult,
+                op1=ALU.mult,
+            )
             products[i] = (by_cos, by_sin)
 
         def rope_transpose(i):
@@ -160,15 +175,47 @@ def tile_bidirectionalattentionv2_pa_t_kernel(tc, Q, V, rope_cos, rope_sin, out)
 
         v_grouped = {}
 
-        def v_group(h, g):
-            v_grouped[h, g] = grouped_pool.tile([P, N, 2, 2], BF16, name="v_grouped", align_bytes=64)
-            nc.vector.tensor_copy(out=v_grouped[h, g][:], in_=v_sb[h][:, g].rearrange("p (e a) n -> p n a e", a=2))
+        def v_group(h, g, half=None):
+            if (h, g) not in v_grouped:
+                v_grouped[h, g] = v_pool.tile([P, N, 2, 2], BF16, name="v_grouped", tag="v_grouped", align_bytes=64)
+            rows = v_sb[h][:, g].rearrange("p (e a) n -> p n a e", a=2)
+            if half is None:
+                nc.vector.tensor_copy(out=v_grouped[h, g][:], in_=rows)
+            else:
+                columns = slice(N // 2 * half, N // 2 * (half + 1))
+                nc.scalar.copy(out=v_grouped[h, g][:, columns], in_=rows[:, columns])
 
         def v_quantise(h, g):
             nc.vector.quantize_mx(
                 out=v_codes[h][:, g, :].bitcast(FP8X4),
                 scales=v_scales[h][:, g, :],
                 in_=v_grouped[h, g][:].rearrange("p n a e -> p (n a e)"),
+            )
+
+        v_piece = {}
+
+        def piece_place(k):
+            width = PASSES * N // V_PIECES
+            return k * width // N, slice(k * width % N, k * width % N + width)
+
+        def v_piece_group(k):
+            g, columns = piece_place(k)
+            v_piece[k] = strip_pool.tile([P, PASSES * N // V_PIECES, 2, 2], BF16, name="v_piece", tag="shared", align_bytes=64)
+            nc.gpsimd.tensor_scalar(
+                out=v_piece[k][:],
+                in0=v_sb[HEADS - 1][:, g, :, columns].rearrange("p (e a) n -> p n a e", a=2),
+                scalar1=1.0,
+                scalar2=0.0,
+                op0=ALU.mult,
+                op1=ALU.add,
+            )
+
+        def v_piece_quantise(k):
+            g, columns = piece_place(k)
+            nc.vector.quantize_mx(
+                out=v_codes[HEADS - 1][:, g, columns].bitcast(FP8X4),
+                scales=v_scales[HEADS - 1][:, g, columns],
+                in_=v_piece[k][:].rearrange("p n a e -> p (n a e)"),
             )
 
         scores = {}
@@ -262,11 +309,19 @@ def tile_bidirectionalattentionv2_pa_t_kernel(tc, Q, V, rope_cos, rope_sin, out)
                     stop=(g == PASSES - 1),
                 )
 
+        def on_vector(i):
+            return i % 2 == 1 or i + STRIP_STAGES - 1 > STRIPS
+
         def strip_out(i):
             h, b, a = place(i)
             if a == 0:
                 result[h, b] = strip_pool.tile([P, 2, N], F32, name="result")
-            nc.scalar.activation(out=result[h, b][:, a, :], in_=acc[i][:], func=ACT.Copy, scale=inv_sum[i][:])
+            if on_vector(i):
+                nc.vector.tensor_scalar(
+                    out=result[h, b][:, a, :], in0=acc[i][:], scalar1=inv_sum[i][:], scalar2=None, op0=ALU.mult
+                )
+            else:
+                nc.scalar.activation(out=result[h, b][:, a, :], in_=acc[i][:], func=ACT.Copy, scale=inv_sum[i][:])
             if a == 1:
                 nc.sync.dma_start(
                     out=out_rows[h * T + 256 * b : h * T + 256 * (b + 1), :].rearrange("(y a) n -> y (a n)", a=2),
@@ -278,20 +333,31 @@ def tile_bidirectionalattentionv2_pa_t_kernel(tc, Q, V, rope_cos, rope_sin, out)
 
         for r in range(-ROPE_LEAD, STRIPS + STRIP_STAGES - 1):
             tile_i = r + ROPE_LEAD
-            if tile_i < TILES and tile_i % 2 == 0:
-                sign_sine(tile_i // 2)
-            if is_strip(r - 7):
+            if is_strip(r - 7) and not on_vector(r - 7):
                 strip_out(r - 7)
             if is_strip(r - 4):
                 strip_group(r - 4)
             if is_strip(tile_i - 2):
                 rope_group(tile_i - 2)
+            piece = r - V_ROUND
+            if 0 <= piece < 4 * EARLY_V:
+                v_group(piece // 4, piece // 2 % 2, piece % 2)
+            if 1 <= r <= EARLY_V * PASSES:
+                v_quantise((r - 1) // PASSES, (r - 1) % PASSES)
+            piece = r - 1 - V_PIECE_ROUND
+            if 0 <= piece < V_PIECES:
+                v_piece_quantise(piece)
             if is_strip(r - 5):
                 strip_quantise(r - 5)
+            piece = r - V_PIECE_ROUND
+            if 0 <= piece < V_PIECES:
+                v_piece_group(piece)
             if is_strip(r - 2):
                 strip_max(r - 2, 1)
             if is_strip(r - 1):
                 strip_max(r - 1, 0)
+            if is_strip(r - 7) and on_vector(r - 7):
+                strip_out(r - 7)
             if is_strip(r - 5):
                 strip_inverse(r - 5)
             if is_strip(r - 2):
@@ -301,10 +367,11 @@ def tile_bidirectionalattentionv2_pa_t_kernel(tc, Q, V, rope_cos, rope_sin, out)
             if is_strip(tile_i):
                 rope_products(tile_i)
             for g in range(PASSES):
-                if is_strip(r) and r % TILES == 2 * g:
-                    v_group(r // TILES, g)
-                if is_strip(r) and r % TILES == 2 * g + 1:
-                    v_quantise(r // TILES, g)
+                for h in range(EARLY_V, HEADS - 1):
+                    if r == h * TILES + 2 * g:
+                        v_group(h, g)
+                    if r == h * TILES + 2 * g + 1:
+                        v_quantise(h, g)
             if is_strip(r):
                 strip_scores(r)
             if is_strip(r - 6):

from contextlib import ExitStack

import concourse.mybir as mybir
from concourse.masks import make_identity

F32 = mybir.dt.float32
BF16 = mybir.dt.bfloat16
U32 = mybir.dt.uint32
U8 = mybir.dt.uint8
FP8X4 = mybir.dt.float8_e4m3fn_x4
ALU = mybir.AluOpType
ACT = mybir.ActivationFunctionType

P = 128
HEADS = 4
T = 1024
N = 512
GROUPS = 4
K_PASS = 512
PASSES = T // K_PASS
SCORE_SCALE = 1.0 / 512.0**0.5
TILES = T // P
STRIPS = HEADS * TILES

ROPE_STAGES = 4
ROPE_LEAD = TILES - 1 + ROPE_STAGES
STRIP_STAGES = 8

EARLY_V = 2
V_ROUND = -7

GPSIMD_FROM = ROPE_LEAD + 1
E_SHARED_FROM = ROPE_LEAD + 5
V_PIECE_ROUND = STRIPS - ROPE_LEAD
V_PIECES = 4

FLOPS = 2 * 2 * HEADS * T * T * N


def tile_bidirectionalattentionv2_pa_t_kernel(tc, Q, V, rope_cos, rope_sin, out):
    nc = tc.nc
    q_rows = Q.flatten_outer_dims()
    v_rows = V.flatten_outer_dims()
    cos_rows = rope_cos.flatten_outer_dims()
    sin_rows = rope_sin.flatten_outer_dims()
    out_rows = out.flatten_outer_dims()

    with ExitStack() as stack:
        const = stack.enter_context(tc.tile_pool(name="const", bufs=1))
        keep = stack.enter_context(tc.tile_pool(name="keep", bufs=1))
        rope_pool = stack.enter_context(tc.tile_pool(name="rope", bufs=3))
        grouped_pool = stack.enter_context(tc.tile_pool(name="grouped", bufs=2))
        v_pool = stack.enter_context(tc.tile_pool(name="v_grouped", bufs=4))
        strip_pool = stack.enter_context(tc.tile_pool(name="strip", bufs=3))
        small = stack.enter_context(tc.tile_pool(name="small", bufs=8))
        psum_scores = stack.enter_context(tc.psum_pool(name="psum_scores", bufs=4))
        psum_turned = stack.enter_context(tc.psum_pool(name="psum_turned", bufs=2))
        psum_acc = stack.enter_context(tc.psum_pool(name="psum_acc", bufs=2))
        stack.enter_context(tc.manual_schedule())

        ident = const.tile([P, P], F32)
        make_identity(nc, ident[:])

        cos_sb = const.tile([P, GROUPS, 2, N], BF16)
        sin_sb = const.tile([P, GROUPS, 2, N], BF16)
        q_sb = [keep.tile([P, GROUPS, 2, N], BF16, name="q%d" % h) for h in range(HEADS)]
        v_sb = [keep.tile([P, PASSES, 4, N], BF16, name="v%d" % h) for h in range(HEADS)]

        def load_group(tile_ap, rows, first_row, b):
            nc.sync.dma_start(
                out=tile_ap[:, b].rearrange("p a n -> p (a n)"),
                in_=rows[first_row + 256 * b : first_row + 256 * (b + 1), :].rearrange(
                    "(y a) n -> y (a n)", a=2
                ),
            )

        def load_v(h, g):
            nc.sync.dma_start(
                out=v_sb[h][:, g].rearrange("p t n -> p (t n)"),
                in_=v_rows[h * T + K_PASS * g : h * T + K_PASS * (g + 1), :].rearrange("(p t) n -> p (t n)", t=4),
            )

        for b in range(GROUPS):
            load_group(q_sb[0], q_rows, 0, b)
            load_group(cos_sb, cos_rows, 0, b)
            load_group(sin_sb, sin_rows, 0, b)
            if 1 <= b <= PASSES:
                load_v(0, b - 1)
        for h in range(1, HEADS):
            for b in range(GROUPS):
                load_group(q_sb[h], q_rows, h * T, b)
                if b < PASSES:
                    load_v(h, b)

        qr_codes = [keep.tile([P, T], U32, name="qr_codes%d" % h, align_bytes=64) for h in range(HEADS)]
        qr_scales = [keep.tile([P, T], U8, name="qr_scales%d" % h, align_bytes=64) for h in range(HEADS)]
        v_codes = [
            keep.tile([P, PASSES, N], U32, name="v_codes%d" % h, align_bytes=64) for h in range(HEADS)
        ]
        v_scales = [
            keep.tile([P, PASSES, N], U8, name="v_scales%d" % h, align_bytes=64) for h in range(HEADS)
        ]

        def place(i):
            return i // TILES, (i % TILES) // 2, i % 2

        products = {}
        qr_turned = {}
        qr_grouped = {}

        def rope_products(i):
            h, b, a = place(i)
            q_blocks = q_sb[h][:, b, a].rearrange("p (k i t) -> p k t i", i=4, t=4)
            cos_blocks = cos_sb[:, b, a].rearrange("p (k i t) -> p k t i", i=4, t=4)
            sin_blocks = sin_sb[:, b, a].rearrange("p (k i t) -> p k t i", i=4, t=4)
            if i < GPSIMD_FROM:
                cos_engine = nc.vector
                by_cos = rope_pool.tile([P, 4, P], F32, name="by_cos")
            else:
                cos_engine = nc.gpsimd
                pool, tag = (v_pool, "v_grouped") if i < E_SHARED_FROM else (strip_pool, "shared")
                by_cos = pool.tile([P, 4, P], F32, name="by_cos_" + tag, tag=tag, align_bytes=64)
            by_sin = rope_pool.tile([P, 4, P], F32)
            by_cos_blocks = by_cos[:].rearrange("p t (k i) -> p k t i", i=4)
            by_sin_blocks = by_sin[:].rearrange("p t (k i) -> p k t i", i=4)
            cos_engine.tensor_tensor(out=by_cos_blocks, in0=q_blocks, in1=cos_blocks, op=ALU.mult)
            nc.vector.tensor_tensor(
                out=by_sin_blocks[:, :, 1::2, :],
                in0=q_blocks[:, :, 0::2, :],
                in1=sin_blocks[:, :, 1::2, :],
                op=ALU.mult,
            )
            q_planes = q_sb[h][:, b, a].rearrange("p (w t) -> p t w", t=4)
            sin_planes = sin_sb[:, b, a].rearrange("p (w t) -> p t w", t=4)
            nc.vector.scalar_tensor_tensor(
                out=by_sin[:, 0::2, :],
                in0=q_planes[:, 1::2, :],
                scalar=-1.0,
                in1=sin_planes[:, 0::2, :],
                op0=ALU.mult,
                op1=ALU.mult,
            )
            products[i] = (by_cos, by_sin)

        def rope_transpose(i):
            by_cos, by_sin = products[i]
            turned = psum_turned.tile([P, 4, P], F32, name="turned")
            for t in range(4):
                nc.tensor.matmul(
                    out=turned[:, t, :], lhsT=by_cos[:, t, :], rhs=ident[:], start=True, stop=False, is_transpose=True
                )
                nc.tensor.matmul(
                    out=turned[:, t, :], lhsT=by_sin[:, t, :], rhs=ident[:], start=False, stop=True, is_transpose=True
                )
            qr_turned[i] = turned

        def rope_group(i):
            h, b, a = place(i)
            if i % TILES == 0:
                qr_grouped[h] = grouped_pool.tile([P, 4 * T], BF16, name="qr_grouped", align_bytes=64)
            columns = qr_grouped[h][:].rearrange(
                "p (g a half y t) -> p g a half y t", g=PASSES, a=2, half=2, t=4
            )
            nc.scalar.copy(out=columns[:, b // 2, a, b % 2], in_=qr_turned[i][:].rearrange("p t y -> p y t"))

        def rope_quantise(i):
            h, b, a = place(i)
            if (b % 2, a) == (1, 1):
                g = b // 2
                nc.vector.quantize_mx(
                    out=qr_codes[h][:, K_PASS * g : K_PASS * (g + 1)].bitcast(FP8X4),
                    scales=qr_scales[h][:, K_PASS * g : K_PASS * (g + 1)],
                    in_=qr_grouped[h][:, 4 * K_PASS * g : 4 * K_PASS * (g + 1)],
                )

        v_grouped = {}

        def v_group(h, g, half=None):
            if (h, g) not in v_grouped:
                v_grouped[h, g] = v_pool.tile([P, N, 2, 2], BF16, name="v_grouped", tag="v_grouped", align_bytes=64)
            rows = v_sb[h][:, g].rearrange("p (e a) n -> p n a e", a=2)
            if half is None:
                nc.vector.tensor_copy(out=v_grouped[h, g][:], in_=rows)
            else:
                columns = slice(N // 2 * half, N // 2 * (half + 1))
                nc.scalar.copy(out=v_grouped[h, g][:, columns], in_=rows[:, columns])

        def v_quantise(h, g):
            nc.vector.quantize_mx(
                out=v_codes[h][:, g, :].bitcast(FP8X4),
                scales=v_scales[h][:, g, :],
                in_=v_grouped[h, g][:].rearrange("p n a e -> p (n a e)"),
            )

        v_piece = {}

        def piece_place(k):
            width = PASSES * N // V_PIECES
            return k * width // N, slice(k * width % N, k * width % N + width)

        def v_piece_group(k):
            g, columns = piece_place(k)
            v_piece[k] = strip_pool.tile([P, PASSES * N // V_PIECES, 2, 2], BF16, name="v_piece", tag="shared", align_bytes=64)
            nc.gpsimd.tensor_scalar(
                out=v_piece[k][:],
                in0=v_sb[HEADS - 1][:, g, :, columns].rearrange("p (e a) n -> p n a e", a=2),
                scalar1=1.0,
                scalar2=0.0,
                op0=ALU.mult,
                op1=ALU.add,
            )

        def v_piece_quantise(k):
            g, columns = piece_place(k)
            nc.vector.quantize_mx(
                out=v_codes[HEADS - 1][:, g, columns].bitcast(FP8X4),
                scales=v_scales[HEADS - 1][:, g, columns],
                in_=v_piece[k][:].rearrange("p n a e -> p (n a e)"),
            )

        scores = {}
        neg_s = {}
        run_min = {}
        e_sb = {}
        row_sum = {}
        e_turned = {}
        e_grouped = {}
        e_operand = {}
        inv_sum = {}
        acc = {}
        result = {}

        def strip_scores(i):
            h, b, a = place(i)
            first = K_PASS * (b // 2) + 256 * a + P * (b % 2)
            scores[i] = [psum_scores.tile([P, K_PASS], F32, name="scores") for g in range(PASSES)]
            for g in range(PASSES):
                nc.tensor.matmul_mx(
                    out=scores[i][g][:],
                    lhsT=qr_codes[h][:, first : first + P].bitcast(FP8X4),
                    lhsT_scale=qr_scales[h][:, first : first + P],
                    rhs=qr_codes[h][:, K_PASS * g : K_PASS * (g + 1)].bitcast(FP8X4),
                    rhs_scale=qr_scales[h][:, K_PASS * g : K_PASS * (g + 1)],
                    start=True,
                    stop=True,
                )

        def strip_max(i, g):
            if g == 0:
                neg_s[i] = strip_pool.tile([P, T], F32, name="neg_s")
                run_min[i] = small.tile([P, PASSES], F32, name="run_min")
            nc.vector.tensor_scalar(
                out=neg_s[i][:, K_PASS * g : K_PASS * (g + 1)],
                in0=scores[i][g][:],
                scalar1=-SCORE_SCALE,
                scalar2=(None if g == 0 else run_min[i][:, g - 1 : g]),
                op0=ALU.mult,
                op1=ALU.min,
                accum_out=run_min[i][:, g : g + 1],
            )

        def strip_exp(i):
            e_sb[i] = strip_pool.tile([P, T], BF16, name="e_sb")
            row_sum[i] = small.tile([P, 1], F32, name="row_sum")
            nc.scalar.activation(
                out=e_sb[i][:],
                in_=neg_s[i][:],
                func=ACT.Exp,
                bias=run_min[i][:, PASSES - 1 : PASSES],
                scale=-1.0,
                accum_out=row_sum[i][:],
            )

        def strip_transpose(i):
            e_words = e_sb[i][:].bitcast(F32)
            e_turned[i] = psum_turned.tile([P, 2 * PASSES, P], F32, name="turned")
            for j in range(2 * PASSES):
                nc.tensor.transpose(e_turned[i][:, j, :], e_words[:, P * j : P * (j + 1)], ident[:])

        def strip_group(i):
            e_grouped[i] = strip_pool.tile([P, 4 * PASSES * P], BF16, name="e_grouped", tag="shared", align_bytes=64)
            nc.scalar.copy(
                out=e_grouped[i][:].bitcast(F32).rearrange("p (g q a) -> p g q a", g=PASSES, a=2),
                in_=e_turned[i][:].rearrange("p (g a) q -> p g q a", a=2),
            )

        def strip_quantise(i):
            e_codes = strip_pool.tile([P, PASSES * P], U32, align_bytes=64)
            e_scales = strip_pool.tile([P, PASSES * P], U8, align_bytes=64)
            nc.vector.quantize_mx(out=e_codes[:].bitcast(FP8X4), scales=e_scales[:], in_=e_grouped[i][:])
            e_operand[i] = (e_codes, e_scales)

        def strip_inverse(i):
            inv_sum[i] = small.tile([P, 1], F32, name="inv_sum")
            nc.vector.reciprocal(out=inv_sum[i][:], in_=row_sum[i][:])

        def strip_values(i):
            h, b, a = place(i)
            e_codes, e_scales = e_operand[i]
            acc[i] = psum_acc.tile([P, N], F32, name="acc")
            for g in range(PASSES):
                nc.tensor.matmul_mx(
                    out=acc[i][:],
                    lhsT=e_codes[:, P * g : P * (g + 1)].bitcast(FP8X4),
                    lhsT_scale=e_scales[:, P * g : P * (g + 1)],
                    rhs=v_codes[h][:, g, :].bitcast(FP8X4),
                    rhs_scale=v_scales[h][:, g, :],
                    start=(g == 0),
                    stop=(g == PASSES - 1),
                )

        def on_vector(i):
            return i % 2 == 1 or i + STRIP_STAGES - 1 > STRIPS

        def strip_out(i):
            h, b, a = place(i)
            if a == 0:
                result[h, b] = strip_pool.tile([P, 2, N], F32, name="result")
            if on_vector(i):
                nc.vector.tensor_scalar(
                    out=result[h, b][:, a, :], in0=acc[i][:], scalar1=inv_sum[i][:], scalar2=None, op0=ALU.mult
                )
            else:
                nc.scalar.activation(out=result[h, b][:, a, :], in_=acc[i][:], func=ACT.Copy, scale=inv_sum[i][:])
            if a == 1:
                nc.sync.dma_start(
                    out=out_rows[h * T + 256 * b : h * T + 256 * (b + 1), :].rearrange("(y a) n -> y (a n)", a=2),
                    in_=result[h, b][:].rearrange("p a n -> p (a n)"),
                )

        def is_strip(i):
            return 0 <= i < STRIPS

        for r in range(-ROPE_LEAD, STRIPS + STRIP_STAGES - 1):
            tile_i = r + ROPE_LEAD
            if is_strip(r - 7) and not on_vector(r - 7):
                strip_out(r - 7)
            if is_strip(r - 4):
                strip_group(r - 4)
            if is_strip(tile_i - 2):
                rope_group(tile_i - 2)
            piece = r - V_ROUND
            if 0 <= piece < 4 * EARLY_V:
                v_group(piece // 4, piece // 2 % 2, piece % 2)
            if 1 <= r <= EARLY_V * PASSES:
                v_quantise((r - 1) // PASSES, (r - 1) % PASSES)
            piece = r - 1 - V_PIECE_ROUND
            if 0 <= piece < V_PIECES:
                v_piece_quantise(piece)
            if is_strip(r - 5):
                strip_quantise(r - 5)
            piece = r - V_PIECE_ROUND
            if 0 <= piece < V_PIECES:
                v_piece_group(piece)
            if is_strip(r - 2):
                strip_max(r - 2, 1)
            if is_strip(r - 1):
                strip_max(r - 1, 0)
            if is_strip(r - 7) and on_vector(r - 7):
                strip_out(r - 7)
            if is_strip(r - 5):
                strip_inverse(r - 5)
            if is_strip(r - 2):
                strip_exp(r - 2)
            if is_strip(tile_i - 3):
                rope_quantise(tile_i - 3)
            if is_strip(tile_i):
                rope_products(tile_i)
            for g in range(PASSES):
                for h in range(EARLY_V, HEADS - 1):
                    if r == h * TILES + 2 * g:
                        v_group(h, g)
                    if r == h * TILES + 2 * g + 1:
                        v_quantise(h, g)
            if is_strip(r):
                strip_scores(r)
            if is_strip(r - 6):
                strip_values(r - 6)
            if is_strip(r - 3):
                strip_transpose(r - 3)
            if is_strip(tile_i - 1):
                rope_transpose(tile_i - 1)
